import numpy as np
import ml_dtypes


def mxq(x, axis, fmt="e4m3"):
    dtype, down = {"e4m3": (ml_dtypes.float8_e4m3fn, 7), "e5m2": (ml_dtypes.float8_e5m2, 14)}[fmt]
    v = np.moveaxis(np.asarray(x, np.float32).astype(ml_dtypes.bfloat16).astype(np.float64), axis, -1)
    blocks = v.reshape(v.shape[:-1] + (-1, 32))
    amax = np.abs(blocks).max(-1, keepdims=True)
    byte = np.maximum(np.where(amax > 0, np.frexp(amax)[1] - 1 + 127, 0) - down, 1)
    scale = np.exp2(byte - 127.0)
    codes = (blocks / scale).astype(np.float32).astype(dtype).astype(np.float64)
    return np.moveaxis((codes * scale).reshape(v.shape), -1, axis)


WIDE = False


def mx_kscale(k):
    if not WIDE:
        return np.ones(k)
    levels = np.array([20, -20, 10, -10, 0])
    a = np.random.permutation(np.resize(levels, k // 512 * 4)).reshape(k // 512, 4)
    idx = np.arange(k)
    return np.exp2(a[idx // 512, idx % 128 // 32])


BF16 = ml_dtypes.bfloat16


def bf(x):
    return np.asarray(x, np.float32).astype(BF16)


def f64(x):
    return np.asarray(x).astype(np.float64)


N, E, D = 2048, 2048, 512


def setup_inputs():
    u = mx_kscale(D)
    X = np.random.standard_normal((N, D)) * 0.5 * np.sqrt(N) * u
    H = np.random.uniform(0.0, 1.0, (N, E)) * (16.0 / N)
    g = np.random.standard_normal((E, D)) * np.exp2(np.random.randint(-12, 1, (E, 1))) / u
    return {"X": bf(X), "H": bf(H), "grad_out": bf(g)}


def reference(X, H, grad_out):
    Hf = f64(H)
    P = mxq(f64(X), 1, "e4m3") @ mxq(f64(grad_out), 1, "e5m2").T
    with np.errstate(divide="ignore"):
        inv_deg = 1.0 / Hf.sum(axis=0)
    inv_deg = np.where(np.isinf(inv_deg), 0.0, inv_deg)
    c = (Hf * P).sum(axis=0)
    return (P - (c * inv_deg)[None, :]) * inv_deg[None, :]

@@ -1,0 +1,415 @@
+from contextlib import ExitStack
+
+import concourse.mybir as mybir
+from concourse.masks import make_identity
+
+F32 = mybir.dt.float32
+BF16 = mybir.dt.bfloat16
+U32 = mybir.dt.uint32
+U8 = mybir.dt.uint8
+E4M3X4 = mybir.dt.float8_e4m3fn_x4
+E5M2X4 = mybir.dt.float8_e5m2_x4
+ALU = mybir.AluOpType
+ACT = mybir.ActivationFunctionType
+AX = mybir.AxisListType
+
+P = 128
+NV = 2048
+NE = 2048
+D = 512
+FLOPS = 2 * NV * NE * D
+
+H_CHUNKS = (
+    (0, 8, 0, 256),
+    (8, 16, 0, 256),
+    (0, 16, 256, 512),
+    (0, 16, 512, 1024),
+    (0, 16, 1024, 2048),
+)
+ROUNDS = ((0, 2), (2, 4), (4, 8), (8, 16))
+DEG_AT = {4: (2,), 5: (3,), 8: (4, 5), 9: (6, 7), 14: (8, 9), 15: (10, 11), 16: (12, 13), 17: (14, 15)}
+CHAIN_AT = {5: 1, 9: 2, 17: 3}
+SEL_AT = {6: 1, 10: 2, 18: 3}
+HALF_AT = {7: 1, 11: 2, 19: 3}
+GPREP_AT = {4: 1, 10: 2, 12: 3}
+GQUANT_AT = {5: 1, 11: 2, 13: 3}
+TAIL_IDX = 52
+TAIL_TAGS = ("o0", "o1", "pt0", "pt1")
+
+
+def tile_v2emsgpass_kernel(tc, X, H, grad_out, out):
+    nc = tc.nc
+    with ExitStack() as ctx:
+        const = ctx.enter_context(tc.tile_pool(name="const", bufs=1))
+        hpool = ctx.enter_context(tc.tile_pool(name="hpool", bufs=1))
+        rawp = ctx.enter_context(tc.tile_pool(name="rawp", bufs=4))
+        grpp = ctx.enter_context(tc.tile_pool(name="grpp", bufs=3))
+        ptp = ctx.enter_context(tc.tile_pool(name="ptp", bufs=3))
+        outp = ctx.enter_context(tc.tile_pool(name="outp", bufs=2))
+        psum = ctx.enter_context(tc.psum_pool(name="psum", bufs=1))
+        ctx.enter_context(tc.manual_schedule())
+
+        xv = X.rearrange("(p t) d -> p t d", t=16)
+        gv = grad_out.rearrange("(b q r) d -> q b r d", q=P, r=2)
+        hv = H.rearrange("(p t) e -> p t e", t=16)
+        ov = out.rearrange("(p t) e -> p t e", t=16)
+
+        ident = const.tile([P, P], F32, name="ident")
+        make_identity(nc, ident[:])
+        ones = const.tile([P, 16], BF16, name="ones")
+        nc.vector.memset(ones[:], 1.0)
+        rhs_sb = const.tile([P, 2, 16], F32, name="rhs_sb")
+        nc.vector.memset(rhs_sb[:], 0.0)
+        sel = [const.tile([P, P], F32, name="sel%d" % r) for r in range(2)]
+        idv = ident[:].rearrange("p (q r) -> p q r", r=2)
+        for r in range(2):
+            for hf in range(2):
+                nc.vector.tensor_copy(out=sel[r][:, hf * 64 : (hf + 1) * 64], in_=idv[:, :, r])
+
+        junk = const.tile([P, 512], F32, name="junk")
+        zero_mask = const.tile([P, 16], F32, name="zero_mask")
+        safe_deg = const.tile([P, 16], F32, name="safe_deg")
+        recip = const.tile([P, 16], F32, name="recip")
+        scal = const.tile([P, 8, 2, 2], F32, name="scal")
+        c4 = const.tile([P, 8, 2, 4], F32, name="c4")
+        csum = const.tile([P, 8, 2], F32, name="csum")
+        bias = const.tile([P, 8, 2], F32, name="bias")
+        codes = {
+            "x": const.tile([P, NV], U32, name="x_codes", align_bytes=64),
+            "g": const.tile([P, NE], U32, name="g_codes", align_bytes=64),
+        }
+        scales = {
+            "x": const.tile([P, NV], U8, name="x_scales", align_bytes=64),
+            "g": const.tile([P, NE], U8, name="g_scales", align_bytes=64),
+        }
+        fmt = {"x": E4M3X4, "g": E5M2X4}
+        dbank = psum.tile([P, 512], F32, tag="d", name="dbank")
+
+        raw = {}
+        grouped = {}
+        prep_bank = {}
+        h_tiles = {}
+        pt = {}
+        ht = {}
+        ptsb = {}
+        obank = {}
+        osb = {}
+
+        def evac(engine, dst, src):
+            if engine == "S":
+                nc.scalar.copy(out=dst, in_=src)
+            else:
+                nc.vector.tensor_copy(out=dst, in_=src)
+
+        def load_rows(kind, i):
+            t = rawp.tile([P, 4, D], BF16, name="raw_%s%d" % (kind, i), tag="raw")
+            if kind == "x":
+                nc.sync.dma_start(out=t[:], in_=xv[:, 4 * i : 4 * i + 4, :])
+            else:
+                nc.sync.dma_start(
+                    out=t[:].rearrange("q (b r) d -> q b r d", b=2),
+                    in_=gv[:, 2 * i : 2 * i + 2, :, :],
+                )
+            raw[(kind, i)] = t
+
+        def load_h(i):
+            t0, t1, e0, e1 = H_CHUNKS[i]
+            t = hpool.tile([P, t1 - t0, e1 - e0], BF16, name="h%d" % i)
+            nc.sync.dma_start(out=t[:], in_=hv[:, t0:t1, e0:e1])
+            h_tiles[i] = t
+
+        def h_at(b, t):
+            found = None
+            for i, (t0, t1, e0, e1) in enumerate(H_CHUNKS):
+                if t0 <= t < t1 and e0 <= 256 * b < e1:
+                    found = (h_tiles[i], t - t0, 256 * b - e0)
+            return found
+
+        def prep_transposes(kind, i, tags):
+            words = raw[(kind, i)][:].bitcast(F32)
+            for h in range(2):
+                bank = psum.tile([P, 2, 2, P], F32, tag=tags[h], name="prep_%s%d_%d" % (kind, i, h))
+                for r in range(2):
+                    for u in range(2):
+                        nc.tensor.transpose(bank[:, r, u, :], words[:, 2 * h + r, u * P : (u + 1) * P], ident[:])
+                prep_bank[(kind, i, h)] = bank
+
+        def prep_copy(kind, i, h, engine):
+            if h == 0:
+                grouped[(kind, i)] = grpp.tile(
+                    [P, 2048], BF16, name="grp_%s%d" % (kind, i), tag="grp", align_bytes=64
+                )
+            dst = grouped[(kind, i)][:].bitcast(F32).rearrange("w (r c u) -> w r c u", r=4, u=2)
+            evac(engine, dst[:, 2 * h : 2 * h + 2], prep_bank[(kind, i, h)][:].rearrange("w r u c -> w r c u"))
+
+        def quantise(kind, i):
+            cols = slice(i * 512, (i + 1) * 512)
+            nc.vector.quantize_mx(
+                out=codes[kind][:, cols].bitcast(fmt[kind]),
+                scales=scales[kind][:, cols],
+                in_=grouped[(kind, i)][:],
+            )
+
+        def mx(s):
+            b, nb = divmod(s, 4)
+            for par in range(2):
+                bank = psum.tile([P, 512], F32, tag="pt%d" % par, name="pt_%d_%d" % (s, par))
+                ecols = slice(b * 256 + par * P, b * 256 + (par + 1) * P)
+                ncols = slice(nb * 512, (nb + 1) * 512)
+                nc.tensor.matmul_mx(
+                    out=bank[:],
+                    lhsT=codes["g"][:, ecols].bitcast(E5M2X4),
+                    lhsT_scale=scales["g"][:, ecols],
+                    rhs=codes["x"][:, ncols].bitcast(E4M3X4),
+                    rhs_scale=scales["x"][:, ncols],
+                    start=True,
+                    stop=True,
+                )
+                pt[(s, par)] = bank
+
+        def ptcopy(s):
+            b, nb = divmod(s, 4)
+            if nb == 0:
+                ptsb[b] = ptp.tile([P, 2, NV], F32, name="ptsb%d" % b, tag="ptsb")
+            for par in range(2):
+                nc.scalar.copy(out=ptsb[b][:, par, nb * 512 : (nb + 1) * 512], in_=pt[(s, par)][:])
+
+        def h_transposes(u):
+            b, nb = divmod(u, 4)
+            bank = psum.tile([P, 512], F32, tag="ht%d" % (u % 3), name="ht_%d" % u)
+            for tl in range(4):
+                tile_, tloc, off = h_at(b, 4 * nb + tl)
+                words = tile_[:].bitcast(F32)
+                nc.tensor.transpose(
+                    bank[:, tl * P : (tl + 1) * P], words[:, tloc, off // 2 : off // 2 + P], ident[:]
+                )
+            ht[u] = bank
+
+        def weighted_sums(s):
+            b, nb = divmod(s, 4)
+            hview = ht[s][:].bitcast(BF16).rearrange("q (n r) -> q n r", r=2)
+            for par in range(2):
+                nc.vector.scalar_tensor_tensor(
+                    out=junk[:],
+                    in0=hview[:, :, par],
+                    scalar=1.0,
+                    in1=ptsb[b][:, par, nb * 512 : (nb + 1) * 512],
+                    op0=ALU.mult,
+                    op1=ALU.mult,
+                    accum_out=c4[:, b, par, nb : nb + 1],
+                )
+
+        def degree_group(j):
+            b, jj = divmod(j, 2)
+            for t in range(16):
+                tile_, tloc, off = h_at(b, t)
+                nc.tensor.matmul(
+                    out=dbank[:, j * 16 : (j + 1) * 16],
+                    lhsT=tile_[:, tloc, off + jj * P : off + (jj + 1) * P],
+                    rhs=ones[:],
+                    start=(t == 0),
+                    stop=(t == 15),
+                )
+
+        def chain(rd):
+            j0, j1 = ROUNDS[rd]
+            deg = dbank[:, 0:256].rearrange("p (j n) -> p j n", n=16)[:, j0:j1, 0]
+            nc.vector.tensor_single_scalar(out=zero_mask[:, j0:j1], in_=deg, scalar=0.0, op=ALU.is_equal)
+            nc.vector.tensor_tensor(out=safe_deg[:, j0:j1], in0=deg, in1=zero_mask[:, j0:j1], op=ALU.add)
+            nc.vector.reciprocal(out=recip[:, j0:j1], in_=safe_deg[:, j0:j1])
+            nc.vector.scalar_tensor_tensor(
+                out=rhs_sb[:, 0, j0:j1],
+                in0=zero_mask[:, j0:j1],
+                scalar=0.0,
+                in1=recip[:, j0:j1],
+                op0=ALU.is_equal,
+                op1=ALU.mult,
+            )
+            nc.vector.scalar_tensor_tensor(
+                out=rhs_sb[:, 1, j0:j1],
+                in0=rhs_sb[:, 0, j0:j1],
+                scalar=-1.0,
+                in1=rhs_sb[:, 0, j0:j1],
+                op0=ALU.mult,
+                op1=ALU.mult,
+            )
+
+        def select(rd):
+            for par in range(2):
+                lo = 256 + rd * 64 + par * 32
+                nc.tensor.matmul(
+                    out=dbank[:, lo : lo + 32],
+                    lhsT=sel[par][:],
+                    rhs=rhs_sb[:].rearrange("p k j -> p (k j)"),
+                    start=True,
+                    stop=True,
+                )
+
+        def half_copies(rd):
+            c0, c1 = ROUNDS[rd][0] // 2, ROUNDS[rd][1] // 2
+            lo = 256 + rd * 64
+            for hf in range(2):
+                rows = slice(hf * 64, (hf + 1) * 64)
+                src = dbank[rows, lo : lo + 64].rearrange("q (r k c w) -> q r k c w", r=2, k=2, c=8, w=2)
+                nc.scalar.copy(
+                    out=scal[rows, c0:c1, :, :].rearrange("q c r k -> q r k c"),
+                    in_=src[:, :, :, c0:c1, hf],
+                )
+
+        def make_bias(b):
+            nc.vector.tensor_reduce(out=csum[:, b, :], in_=c4[:, b, :, :], axis=AX.X, op=ALU.add)
+            nc.vector.tensor_tensor(out=bias[:, b, :], in0=csum[:, b, :], in1=scal[:, b, :, 1], op=ALU.mult)
+
+        def affine(b):
+            if b < 7:
+                for h in range(2):
+                    for par in range(2):
+                        seg = ptsb[b][:, par, h * 1024 : (h + 1) * 1024]
+                        nc.gpsimd.tensor_scalar(
+                            out=seg,
+                            in0=seg,
+                            scalar1=scal[:, b, par, 0:1],
+                            scalar2=bias[:, b, par : par + 1],
+                            op0=ALU.mult,
+                            op1=ALU.add,
+                        )
+            else:
+                for h in range(4):
+                    for par in range(2):
+                        seg = ptsb[b][:, par, h * 512 : (h + 1) * 512]
+                        nc.vector.tensor_scalar(
+                            out=seg,
+                            in0=seg,
+                            scalar1=scal[:, b, par, 0:1],
+                            scalar2=bias[:, b, par : par + 1],
+                            op0=ALU.mult,
+                            op1=ALU.add,
+                        )
+
+        def back_transposes(idx):
+            b, k = divmod(idx, 8)
+            tag = "o%d" % (idx % 2) if idx < TAIL_IDX else TAIL_TAGS[idx % 4]
+            bank = psum.tile([P, 2, 2, P], F32, tag=tag, name="o_%d" % idx)
+            for tl in range(2):
+                for par in range(2):
+                    t = 2 * k + tl
+                    nc.tensor.transpose(bank[:, tl, par, :], ptsb[b][:, par, t * P : (t + 1) * P], ident[:])
+            obank[idx] = bank
+
+        def store(pair, t0, t1):
+            nc.sync.dma_start(out=ov[:, t0:t1, pair * 512 : (pair + 1) * 512], in_=osb[pair][:, t0:t1, :])
+
+        def out_copy(idx):
+            b, k = divmod(idx, 8)
+            pair, half = divmod(b, 2)
+            if idx < TAIL_IDX:
+                engine = "V" if idx % 4 == 3 else "S"
+            elif idx < TAIL_IDX + 6:
+                engine = "S"
+            else:
+                engine = "V" if idx % 2 == 0 else "S"
+            if half == 0 and k == 0:
+                osb[pair] = outp.tile([P, 16, 512], F32, name="osb%d" % pair, tag="osb")
+            dst = osb[pair][:, 2 * k : 2 * k + 2, half * 256 : (half + 1) * 256]
+            evac(engine, dst.rearrange("p t (q r) -> p t q r", r=2), obank[idx][:].rearrange("p t r q -> p t q r"))
+            if half == 1:
+                if pair < 3:
+                    if k == 3:
+                        store(pair, 0, 8)
+                    if k == 7:
+                        store(pair, 8, 16)
+                else:
+                    if k in (1, 3, 5):
+                        store(pair, 2 * k - 2, 2 * k + 2)
+                    if k in (6, 7):
+                        store(pair, 2 * k, 2 * k + 2)
+
+        load_rows("x", 0)
+        load_rows("g", 0)
+        load_rows("x", 1)
+        load_h(0)
+        load_rows("x", 2)
+        prep_transposes("x", 0, ("o0", "o1"))
+        load_rows("x", 3)
+        load_h(1)
+        load_h(2)
+        prep_copy("x", 0, 0, "S")
+        prep_copy("x", 0, 1, "V")
+        prep_transposes("g", 0, ("pt0", "pt1"))
+        load_rows("g", 1)
+        load_h(3)
+        prep_copy("g", 0, 0, "S")
+        prep_copy("g", 0, 1, "V")
+        quantise("x", 0)
+        prep_transposes("x", 1, ("o0", "o1"))
+        load_rows("g", 2)
+        prep_copy("x", 1, 0, "S")
+        prep_copy("x", 1, 1, "V")
+        quantise("g", 0)
+        quantise("x", 1)
+        mx(0)
+        ptcopy(0)
+        h_transposes(0)
+        h_transposes(1)
+        weighted_sums(0)
+        prep_transposes("x", 2, ("o0", "o1"))
+        load_rows("g", 3)
+        load_h(4)
+        prep_copy("x", 2, 0, "S")
+        prep_copy("x", 2, 1, "S")
+        quantise("x", 2)
+        mx(1)
+        ptcopy(1)
+        weighted_sums(1)
+        prep_transposes("x", 3, ("o0", "o1"))
+        prep_copy("x", 3, 0, "S")
+        prep_copy("x", 3, 1, "S")
+        quantise("x", 3)
+        mx(2)
+        ptcopy(2)
+        h_transposes(2)
+        weighted_sums(2)
+        degree_group(0)
+        degree_group(1)
+        chain(0)
+        mx(3)
+        ptcopy(3)
+        h_transposes(3)
+        h_transposes(4)
+        select(0)
+        half_copies(0)
+        weighted_sums(3)
+        make_bias(0)
+        affine(0)
+
+        for s in range(4, 38):
+            if s < 32:
+                mx(s)
+                ptcopy(s)
+            if s in HALF_AT:
+                half_copies(HALF_AT[s])
+            todo = [idx for idx in ((s - 6) * 2, (s - 6) * 2 + 1) if 0 <= idx < 64]
+            for idx in todo:
+                back_transposes(idx)
+            for j in DEG_AT.get(s, ()):
+                degree_group(j)
+            if s + 1 < 32:
+                h_transposes(s + 1)
+            if s in SEL_AT:
+                select(SEL_AT[s])
+            if s < 32:
+                weighted_sums(s)
+            for idx in todo:
+                out_copy(idx)
+            if s in CHAIN_AT:
+                chain(CHAIN_AT[s])
+            if s < 32 and s % 4 == 3:
+                make_bias(s // 4)
+                affine(s // 4)
+            if s in GPREP_AT:
+                i = GPREP_AT[s]
+                prep_transposes("g", i, ("o0", "o1"))
+                prep_copy("g", i, 0, "S")
+                prep_copy("g", i, 1, "V")
+            if s in GQUANT_AT:
+                quantise("g", GQUANT_AT[s])

@@ -10,7 +10,6 @@ U8 = mybir.dt.uint8
 E4M3X4 = mybir.dt.float8_e4m3fn_x4
 E5M2X4 = mybir.dt.float8_e5m2_x4
 ALU = mybir.AluOpType
-ACT = mybir.ActivationFunctionType
 AX = mybir.AxisListType
 
 P = 128
@@ -26,15 +25,13 @@ H_CHUNKS = (
     (0, 16, 512, 1024),
     (0, 16, 1024, 2048),
 )
-ROUNDS = ((0, 2), (2, 4), (4, 8), (8, 16))
-DEG_AT = {4: (2,), 5: (3,), 8: (4, 5), 9: (6, 7), 14: (8, 9), 15: (10, 11), 16: (12, 13), 17: (14, 15)}
-CHAIN_AT = {5: 1, 9: 2, 17: 3}
-SEL_AT = {6: 1, 10: 2, 18: 3}
-HALF_AT = {7: 1, 11: 2, 19: 3}
-GPREP_AT = {4: 1, 10: 2, 12: 3}
-GQUANT_AT = {5: 1, 11: 2, 13: 3}
+BURST_AT = {4: 1, 7: 2, 10: 3, 14: 4, 18: 5, 22: 6, 26: 7}
+GPREP_AT = {4: 1, 9: 2, 11: 3}
+OT_LAG = 6
+V_COPIES = (1, 5)
 TAIL_IDX = 52
-TAIL_TAGS = ("o0", "o1", "pt0", "pt1")
+TAIL_TAGS = ("o0", "o1", "o2", "pt0", "pt1")
+SPLIT_PAIRS = (2, 3)
 
 
 def tile_v2emsgpass_kernel(tc, X, H, grad_out, out):
@@ -56,20 +53,25 @@ def tile_v2emsgpass_kernel(tc, X, H, grad_out, out):
 
         ident = const.tile([P, P], F32, name="ident")
         make_identity(nc, ident[:])
-        ones = const.tile([P, 16], BF16, name="ones")
+        ones = const.tile([P, 32], BF16, name="ones")
         nc.vector.memset(ones[:], 1.0)
-        rhs_sb = const.tile([P, 2, 16], F32, name="rhs_sb")
-        nc.vector.memset(rhs_sb[:], 0.0)
-        sel = [const.tile([P, P], F32, name="sel%d" % r) for r in range(2)]
+        nsel = [const.tile([P, P], F32, name="nsel%d" % r) for r in range(2)]
         idv = ident[:].rearrange("p (q r) -> p q r", r=2)
         for r in range(2):
             for hf in range(2):
-                nc.vector.tensor_copy(out=sel[r][:, hf * 64 : (hf + 1) * 64], in_=idv[:, :, r])
+                nc.vector.tensor_scalar(
+                    out=nsel[r][:, hf * 64 : (hf + 1) * 64],
+                    in0=idv[:, :, r],
+                    scalar1=-1.0,
+                    scalar2=None,
+                    op0=ALU.mult,
+                )
 
         junk = const.tile([P, 512], F32, name="junk")
-        zero_mask = const.tile([P, 16], F32, name="zero_mask")
-        safe_deg = const.tile([P, 16], F32, name="safe_deg")
-        recip = const.tile([P, 16], F32, name="recip")
+        deg_sb = const.tile([P, 8, 2], F32, name="deg_sb")
+        safe_deg = const.tile([P, 8, 2], F32, name="safe_deg")
+        recip = const.tile([P, 8, 2], F32, name="recip")
+        rhs_sb = const.tile([P, 8, 2, 2], F32, name="rhs_sb")
         scal = const.tile([P, 8, 2, 2], F32, name="scal")
         c4 = const.tile([P, 8, 2, 4], F32, name="c4")
         csum = const.tile([P, 8, 2], F32, name="csum")
@@ -83,7 +85,6 @@ def tile_v2emsgpass_kernel(tc, X, H, grad_out, out):
             "g": const.tile([P, NE], U8, name="g_scales", align_bytes=64),
         }
         fmt = {"x": E4M3X4, "g": E5M2X4}
-        dbank = psum.tile([P, 512], F32, tag="d", name="dbank")
 
         raw = {}
         grouped = {}
@@ -94,6 +95,13 @@ def tile_v2emsgpass_kernel(tc, X, H, grad_out, out):
         ptsb = {}
         obank = {}
         osb = {}
+        selbank = {}
+        uses = [0]
+
+        def next_o_tag():
+            tag = "o%d" % (uses[0] % 3)
+            uses[0] = uses[0] + 1
+            return tag
 
         def evac(engine, dst, src):
             if engine == "S":
@@ -128,7 +136,8 @@ def tile_v2emsgpass_kernel(tc, X, H, grad_out, out):
         def prep_transposes(kind, i, tags):
             words = raw[(kind, i)][:].bitcast(F32)
             for h in range(2):
-                bank = psum.tile([P, 2, 2, P], F32, tag=tags[h], name="prep_%s%d_%d" % (kind, i, h))
+                tag = tags[h] if tags else next_o_tag()
+                bank = psum.tile([P, 2, 2, P], F32, tag=tag, name="prep_%s%d_%d" % (kind, i, h))
                 for r in range(2):
                     for u in range(2):
                         nc.tensor.transpose(bank[:, r, u, :], words[:, 2 * h + r, u * P : (u + 1) * P], ident[:])
@@ -199,62 +208,53 @@ def tile_v2emsgpass_kernel(tc, X, H, grad_out, out):
                     accum_out=c4[:, b, par, nb : nb + 1],
                 )
 
-        def degree_group(j):
-            b, jj = divmod(j, 2)
-            for t in range(16):
-                tile_, tloc, off = h_at(b, t)
-                nc.tensor.matmul(
-                    out=dbank[:, j * 16 : (j + 1) * 16],
-                    lhsT=tile_[:, tloc, off + jj * P : off + (jj + 1) * P],
-                    rhs=ones[:],
-                    start=(t == 0),
-                    stop=(t == 15),
-                )
-
-        def chain(rd):
-            j0, j1 = ROUNDS[rd]
-            deg = dbank[:, 0:256].rearrange("p (j n) -> p j n", n=16)[:, j0:j1, 0]
-            nc.vector.tensor_single_scalar(out=zero_mask[:, j0:j1], in_=deg, scalar=0.0, op=ALU.is_equal)
-            nc.vector.tensor_tensor(out=safe_deg[:, j0:j1], in0=deg, in1=zero_mask[:, j0:j1], op=ALU.add)
-            nc.vector.reciprocal(out=recip[:, j0:j1], in_=safe_deg[:, j0:j1])
-            nc.vector.scalar_tensor_tensor(
-                out=rhs_sb[:, 0, j0:j1],
-                in0=zero_mask[:, j0:j1],
-                scalar=0.0,
-                in1=recip[:, j0:j1],
-                op0=ALU.is_equal,
-                op1=ALU.mult,
-            )
-            nc.vector.scalar_tensor_tensor(
-                out=rhs_sb[:, 1, j0:j1],
-                in0=rhs_sb[:, 0, j0:j1],
-                scalar=-1.0,
-                in1=rhs_sb[:, 0, j0:j1],
-                op0=ALU.mult,
-                op1=ALU.mult,
+        def degree_burst(b):
+            bank = psum.tile([P, 512], F32, tag=next_o_tag(), name="deg_%d" % b)
+            for jj in range(2):
+                for t in range(16):
+                    tile_, tloc, off = h_at(b, t)
+                    nc.tensor.matmul(
+                        out=bank[:, jj * 32 : (jj + 1) * 32],
+                        lhsT=tile_[:, tloc, off + jj * P : off + (jj + 1) * P],
+                        rhs=ones[:],
+                        start=(t == 0),
+                        stop=(t == 15),
+                    )
+            nc.scalar.copy(
+                out=deg_sb[:, b, :], in_=bank[:, 0:64].rearrange("p (j n) -> p j n", n=32)[:, :, 0]
             )
 
-        def select(rd):
+        def chain(b):
+            nc.vector.scalar_tensor_tensor(
+                out=safe_deg[:, b, :], in0=deg_sb[:, b, :], scalar=0.0, in1=deg_sb[:, b, :],
+                op0=ALU.is_equal, op1=ALU.add,
+            )
+            nc.vector.reciprocal(out=recip[:, b, :], in_=safe_deg[:, b, :])
+            nc.vector.scalar_tensor_tensor(
+                out=rhs_sb[:, b, 0, :], in0=deg_sb[:, b, :], scalar=0.0, in1=recip[:, b, :],
+                op0=ALU.is_equal, op1=ALU.subtract,
+            )
+            nc.vector.tensor_tensor(
+                out=rhs_sb[:, b, 1, :], in0=rhs_sb[:, b, 0, :], in1=rhs_sb[:, b, 0, :], op=ALU.mult
+            )
+
+        def select(b):
+            bank = psum.tile([P, 512], F32, tag=next_o_tag(), name="sel_%d" % b)
             for par in range(2):
-                lo = 256 + rd * 64 + par * 32
                 nc.tensor.matmul(
-                    out=dbank[:, lo : lo + 32],
-                    lhsT=sel[par][:],
-                    rhs=rhs_sb[:].rearrange("p k j -> p (k j)"),
+                    out=bank[:, par * 4 : (par + 1) * 4],
+                    lhsT=nsel[par][:],
+                    rhs=rhs_sb[:, b, :, :].rearrange("p k j -> p (k j)"),
                     start=True,
                     stop=True,
                 )
+            selbank[b] = bank
 
-        def half_copies(rd):
-            c0, c1 = ROUNDS[rd][0] // 2, ROUNDS[rd][1] // 2
-            lo = 256 + rd * 64
+        def half_copies(b):
             for hf in range(2):
                 rows = slice(hf * 64, (hf + 1) * 64)
-                src = dbank[rows, lo : lo + 64].rearrange("q (r k c w) -> q r k c w", r=2, k=2, c=8, w=2)
-                nc.scalar.copy(
-                    out=scal[rows, c0:c1, :, :].rearrange("q c r k -> q r k c"),
-                    in_=src[:, :, :, c0:c1, hf],
-                )
+                src = selbank[b][rows, 0:8].rearrange("q (r k j) -> q r k j", r=2, k=2, j=2)
+                nc.scalar.copy(out=scal[rows, b, :, :], in_=src[:, :, :, hf])
 
         def make_bias(b):
             nc.vector.tensor_reduce(out=csum[:, b, :], in_=c4[:, b, :, :], axis=AX.X, op=ALU.add)
@@ -288,7 +288,7 @@ def tile_v2emsgpass_kernel(tc, X, H, grad_out, out):
 
         def back_transposes(idx):
             b, k = divmod(idx, 8)
-            tag = "o%d" % (idx % 2) if idx < TAIL_IDX else TAIL_TAGS[idx % 4]
+            tag = next_o_tag() if idx < TAIL_IDX else TAIL_TAGS[idx % 5]
             bank = psum.tile([P, 2, 2, P], F32, tag=tag, name="o_%d" % idx)
             for tl in range(2):
                 for par in range(2):
@@ -296,14 +296,16 @@ def tile_v2emsgpass_kernel(tc, X, H, grad_out, out):
                     nc.tensor.transpose(bank[:, tl, par, :], ptsb[b][:, par, t * P : (t + 1) * P], ident[:])
             obank[idx] = bank
 
-        def store(pair, t0, t1):
-            nc.sync.dma_start(out=ov[:, t0:t1, pair * 512 : (pair + 1) * 512], in_=osb[pair][:, t0:t1, :])
+        def store(pair, t0, t1, c0, c1):
+            nc.sync.dma_start(
+                out=ov[:, t0:t1, pair * 512 + c0 : pair * 512 + c1], in_=osb[pair][:, t0:t1, c0:c1]
+            )
 
         def out_copy(idx):
             b, k = divmod(idx, 8)
             pair, half = divmod(b, 2)
             if idx < TAIL_IDX:
-                engine = "V" if idx % 4 == 3 else "S"
+                engine = "V" if idx % 8 in V_COPIES else "S"
             elif idx < TAIL_IDX + 6:
                 engine = "S"
             else:
@@ -312,24 +314,26 @@ def tile_v2emsgpass_kernel(tc, X, H, grad_out, out):
                 osb[pair] = outp.tile([P, 16, 512], F32, name="osb%d" % pair, tag="osb")
             dst = osb[pair][:, 2 * k : 2 * k + 2, half * 256 : (half + 1) * 256]
             evac(engine, dst.rearrange("p t (q r) -> p t q r", r=2), obank[idx][:].rearrange("p t r q -> p t q r"))
-            if half == 1:
-                if pair < 3:
-                    if k == 3:
-                        store(pair, 0, 8)
-                    if k == 7:
-                        store(pair, 8, 16)
+            c0 = half * 256
+            if pair in SPLIT_PAIRS:
+                if b < 7:
+                    if k in (3, 7):
+                        store(pair, 2 * k - 6, 2 * k + 2, c0, c0 + 256)
                 else:
                     if k in (1, 3, 5):
-                        store(pair, 2 * k - 2, 2 * k + 2)
+                        store(pair, 2 * k - 2, 2 * k + 2, c0, c0 + 256)
                     if k in (6, 7):
-                        store(pair, 2 * k, 2 * k + 2)
+                        store(pair, 2 * k, 2 * k + 2, c0, c0 + 256)
+            elif half == 1:
+                if k in (3, 7):
+                    store(pair, 2 * k - 6, 2 * k + 2, 0, 512)
 
         load_rows("x", 0)
         load_rows("g", 0)
         load_rows("x", 1)
         load_h(0)
         load_rows("x", 2)
-        prep_transposes("x", 0, ("o0", "o1"))
+        prep_transposes("x", 0, None)
         load_rows("x", 3)
         load_h(1)
         load_h(2)
@@ -341,18 +345,18 @@ def tile_v2emsgpass_kernel(tc, X, H, grad_out, out):
         prep_copy("g", 0, 0, "S")
         prep_copy("g", 0, 1, "V")
         quantise("x", 0)
-        prep_transposes("x", 1, ("o0", "o1"))
+        prep_transposes("x", 1, None)
         load_rows("g", 2)
-        prep_copy("x", 1, 0, "S")
-        prep_copy("x", 1, 1, "V")
         quantise("g", 0)
+        prep_copy("x", 1, 0, "S")
+        prep_copy("x", 1, 1, "S")
         quantise("x", 1)
         mx(0)
         ptcopy(0)
         h_transposes(0)
         h_transposes(1)
         weighted_sums(0)
-        prep_transposes("x", 2, ("o0", "o1"))
+        prep_transposes("x", 2, None)
         load_rows("g", 3)
         load_h(4)
         prep_copy("x", 2, 0, "S")
@@ -361,7 +365,7 @@ def tile_v2emsgpass_kernel(tc, X, H, grad_out, out):
         mx(1)
         ptcopy(1)
         weighted_sums(1)
-        prep_transposes("x", 3, ("o0", "o1"))
+        prep_transposes("x", 3, None)
         prep_copy("x", 3, 0, "S")
         prep_copy("x", 3, 1, "S")
         quantise("x", 3)
@@ -369,8 +373,7 @@ def tile_v2emsgpass_kernel(tc, X, H, grad_out, out):
         ptcopy(2)
         h_transposes(2)
         weighted_sums(2)
-        degree_group(0)
-        degree_group(1)
+        degree_burst(0)
         chain(0)
         mx(3)
         ptcopy(3)
@@ -382,34 +385,34 @@ def tile_v2emsgpass_kernel(tc, X, H, grad_out, out):
         make_bias(0)
         affine(0)
 
-        for s in range(4, 38):
+        for s in range(4, 32 + OT_LAG):
             if s < 32:
                 mx(s)
                 ptcopy(s)
-            if s in HALF_AT:
-                half_copies(HALF_AT[s])
-            todo = [idx for idx in ((s - 6) * 2, (s - 6) * 2 + 1) if 0 <= idx < 64]
+            if s - 2 in BURST_AT:
+                half_copies(BURST_AT[s - 2])
+            if s in BURST_AT:
+                degree_burst(BURST_AT[s])
+            todo = [idx for idx in ((s - OT_LAG) * 2, (s - OT_LAG) * 2 + 1) if 0 <= idx < 64]
             for idx in todo:
                 back_transposes(idx)
-            for j in DEG_AT.get(s, ()):
-                degree_group(j)
             if s + 1 < 32:
                 h_transposes(s + 1)
-            if s in SEL_AT:
-                select(SEL_AT[s])
             if s < 32:
                 weighted_sums(s)
             for idx in todo:
                 out_copy(idx)
-            if s in CHAIN_AT:
-                chain(CHAIN_AT[s])
+            if s in BURST_AT:
+                chain(BURST_AT[s])
+            if s - 1 in BURST_AT:
+                select(BURST_AT[s - 1])
             if s < 32 and s % 4 == 3:
                 make_bias(s // 4)
                 affine(s // 4)
             if s in GPREP_AT:
                 i = GPREP_AT[s]
-                prep_transposes("g", i, ("o0", "o1"))
+                prep_transposes("g", i, None)
                 prep_copy("g", i, 0, "S")
                 prep_copy("g", i, 1, "V")
-            if s in GQUANT_AT:
-                quantise("g", GQUANT_AT[s])
+            if s - 1 in GPREP_AT:
+                quantise("g", GPREP_AT[s - 1])

@@ -25,10 +25,11 @@ H_CHUNKS = (
     (0, 16, 512, 1024),
     (0, 16, 1024, 2048),
 )
-BURST_AT = {4: 1, 7: 2, 10: 3, 14: 4, 18: 5, 22: 6, 26: 7}
+DEG_QUOTA = {(4, "A"): 32, (7, "A"): 12, (7, "B"): 12, (8, "A"): 8}
+DEG_FROM = (8, "B")
 GPREP_AT = {4: 1, 9: 2, 11: 3}
 OT_LAG = 6
-V_COPIES = (1, 5)
+V_COPIES = (1, 3, 5)
 TAIL_IDX = 52
 TAIL_TAGS = ("o0", "o1", "o2", "pt0", "pt1")
 SPLIT_PAIRS = (2, 3)
@@ -97,6 +98,11 @@ def tile_v2emsgpass_kernel(tc, X, H, grad_out, out):
         osb = {}
         selbank = {}
         uses = [0]
+        dbank = psum.tile([P, 512], F32, tag="d", name="dbank")
+        deg_queue = [(b, jj, t) for b in range(1, 8) for jj in range(2) for t in range(16)]
+        chain_at = {}
+        select_at = {}
+        half_at = {}
 
         def next_o_tag():
             tag = "o%d" % (uses[0] % 3)
@@ -185,7 +191,7 @@ def tile_v2emsgpass_kernel(tc, X, H, grad_out, out):
 
         def h_transposes(u):
             b, nb = divmod(u, 4)
-            bank = psum.tile([P, 512], F32, tag="ht%d" % (u % 3), name="ht_%d" % u)
+            bank = psum.tile([P, 512], F32, tag="ht%d" % (u % 2), name="ht_%d" % u)
             for tl in range(4):
                 tile_, tloc, off = h_at(b, 4 * nb + tl)
                 words = tile_[:].bitcast(F32)
@@ -208,21 +214,38 @@ def tile_v2emsgpass_kernel(tc, X, H, grad_out, out):
                     accum_out=c4[:, b, par, nb : nb + 1],
                 )
 
-        def degree_burst(b):
-            bank = psum.tile([P, 512], F32, tag=next_o_tag(), name="deg_%d" % b)
-            for jj in range(2):
-                for t in range(16):
-                    tile_, tloc, off = h_at(b, t)
-                    nc.tensor.matmul(
-                        out=bank[:, jj * 32 : (jj + 1) * 32],
-                        lhsT=tile_[:, tloc, off + jj * P : off + (jj + 1) * P],
-                        rhs=ones[:],
-                        start=(t == 0),
-                        stop=(t == 15),
-                    )
-            nc.scalar.copy(
-                out=deg_sb[:, b, :], in_=bank[:, 0:64].rearrange("p (j n) -> p j n", n=32)[:, :, 0]
+        def degree_matmul(b, jj, t):
+            tile_, tloc, off = h_at(b, t)
+            lo = (b % 2) * 64 + jj * 32
+            nc.tensor.matmul(
+                out=dbank[:, lo : lo + 32],
+                lhsT=tile_[:, tloc, off + jj * P : off + (jj + 1) * P],
+                rhs=ones[:],
+                start=(t == 0),
+                stop=(t == 15),
             )
+
+        def degree_out(b):
+            lo = (b % 2) * 64
+            nc.scalar.copy(
+                out=deg_sb[:, b, :], in_=dbank[:, lo : lo + 64].rearrange("p (j n) -> p j n", n=32)[:, :, 0]
+            )
+
+        def degree_slot(s, which):
+            finished = []
+            count = DEG_QUOTA.get((s, which), 4 if (s, which) >= DEG_FROM else 0)
+            for n in range(count):
+                if deg_queue:
+                    b, jj, t = deg_queue.pop(0)
+                    degree_matmul(b, jj, t)
+                    if jj == 1 and t == 15:
+                        finished.append(b)
+                else:
+                    tile_, tloc, off = h_at(7, 0)
+                    nc.tensor.matmul(
+                        out=dbank[:, 128:160], lhsT=tile_[:, tloc, off : off + P], rhs=ones[:], start=True, stop=True
+                    )
+            return finished
 
         def chain(b):
             nc.vector.scalar_tensor_tensor(
@@ -373,7 +396,10 @@ def tile_v2emsgpass_kernel(tc, X, H, grad_out, out):
         ptcopy(2)
         h_transposes(2)
         weighted_sums(2)
-        degree_burst(0)
+        for jj in range(2):
+            for t in range(16):
+                degree_matmul(0, jj, t)
+        degree_out(0)
         chain(0)
         mx(3)
         ptcopy(3)
@@ -388,11 +414,15 @@ def tile_v2emsgpass_kernel(tc, X, H, grad_out, out):
         for s in range(4, 32 + OT_LAG):
             if s < 32:
                 mx(s)
+                finished = degree_slot(s, "A")
                 ptcopy(s)
-            if s - 2 in BURST_AT:
-                half_copies(BURST_AT[s - 2])
-            if s in BURST_AT:
-                degree_burst(BURST_AT[s])
+                for b in finished:
+                    degree_out(b)
+                    chain_at[s] = b
+                    select_at[s + 1] = b
+                    half_at[s + 2] = b
+            if s in half_at:
+                half_copies(half_at[s])
             todo = [idx for idx in ((s - OT_LAG) * 2, (s - OT_LAG) * 2 + 1) if 0 <= idx < 64]
             for idx in todo:
                 back_transposes(idx)
@@ -402,10 +432,10 @@ def tile_v2emsgpass_kernel(tc, X, H, grad_out, out):
                 weighted_sums(s)
             for idx in todo:
                 out_copy(idx)
-            if s in BURST_AT:
-                chain(BURST_AT[s])
-            if s - 1 in BURST_AT:
-                select(BURST_AT[s - 1])
+            if s in chain_at:
+                chain(chain_at[s])
+            if s in select_at:
+                select(select_at[s])
             if s < 32 and s % 4 == 3:
                 make_bias(s // 4)
                 affine(s // 4)
@@ -416,3 +446,6 @@ def tile_v2emsgpass_kernel(tc, X, H, grad_out, out):
                 prep_copy("g", i, 1, "V")
             if s - 1 in GPREP_AT:
                 quantise("g", GPREP_AT[s - 1])
+            if s < 32:
+                late = degree_slot(s, "B")
+                assert not late

@@ -25,11 +25,11 @@ H_CHUNKS = (
     (0, 16, 512, 1024),
     (0, 16, 1024, 2048),
 )
-DEG_QUOTA = {(4, "A"): 32, (7, "A"): 12, (7, "B"): 12, (8, "A"): 8}
-DEG_FROM = (8, "B")
+ROUNDS = ((0, 1), (1, 2), (2, 4), (4, 8))
+BURST_AT = {4: 1, 7: 2, 14: 3}
 GPREP_AT = {4: 1, 9: 2, 11: 3}
 OT_LAG = 6
-V_COPIES = (1, 3, 5)
+V_COPIES = (1, 5)
 TAIL_IDX = 52
 TAIL_TAGS = ("o0", "o1", "o2", "pt0", "pt1")
 SPLIT_PAIRS = (2, 3)
@@ -56,23 +56,14 @@ def tile_v2emsgpass_kernel(tc, X, H, grad_out, out):
         make_identity(nc, ident[:])
         ones = const.tile([P, 32], BF16, name="ones")
         nc.vector.memset(ones[:], 1.0)
-        nsel = [const.tile([P, P], F32, name="nsel%d" % r) for r in range(2)]
-        idv = ident[:].rearrange("p (q r) -> p q r", r=2)
-        for r in range(2):
-            for hf in range(2):
-                nc.vector.tensor_scalar(
-                    out=nsel[r][:, hf * 64 : (hf + 1) * 64],
-                    in0=idv[:, :, r],
-                    scalar1=-1.0,
-                    scalar2=None,
-                    op0=ALU.mult,
-                )
+        a_pad = const.tile([P, P, 2], F32, name="a_pad")
+        nc.vector.memset(a_pad[:], 0.0)
+        r_sb = const.tile([P, 256], F32, name="r_sb")
 
         junk = const.tile([P, 512], F32, name="junk")
         deg_sb = const.tile([P, 8, 2], F32, name="deg_sb")
         safe_deg = const.tile([P, 8, 2], F32, name="safe_deg")
         recip = const.tile([P, 8, 2], F32, name="recip")
-        rhs_sb = const.tile([P, 8, 2, 2], F32, name="rhs_sb")
         scal = const.tile([P, 8, 2, 2], F32, name="scal")
         c4 = const.tile([P, 8, 2, 4], F32, name="c4")
         csum = const.tile([P, 8, 2], F32, name="csum")
@@ -98,11 +89,6 @@ def tile_v2emsgpass_kernel(tc, X, H, grad_out, out):
         osb = {}
         selbank = {}
         uses = [0]
-        dbank = psum.tile([P, 512], F32, tag="d", name="dbank")
-        deg_queue = [(b, jj, t) for b in range(1, 8) for jj in range(2) for t in range(16)]
-        chain_at = {}
-        select_at = {}
-        half_at = {}
 
         def next_o_tag():
             tag = "o%d" % (uses[0] % 3)
@@ -191,7 +177,7 @@ def tile_v2emsgpass_kernel(tc, X, H, grad_out, out):
 
         def h_transposes(u):
             b, nb = divmod(u, 4)
-            bank = psum.tile([P, 512], F32, tag="ht%d" % (u % 2), name="ht_%d" % u)
+            bank = psum.tile([P, 512], F32, tag="ht%d" % (u % 3), name="ht_%d" % u)
             for tl in range(4):
                 tile_, tloc, off = h_at(b, 4 * nb + tl)
                 words = tile_[:].bitcast(F32)
@@ -214,70 +200,63 @@ def tile_v2emsgpass_kernel(tc, X, H, grad_out, out):
                     accum_out=c4[:, b, par, nb : nb + 1],
                 )
 
-        def degree_matmul(b, jj, t):
-            tile_, tloc, off = h_at(b, t)
-            lo = (b % 2) * 64 + jj * 32
-            nc.tensor.matmul(
-                out=dbank[:, lo : lo + 32],
-                lhsT=tile_[:, tloc, off + jj * P : off + (jj + 1) * P],
-                rhs=ones[:],
-                start=(t == 0),
-                stop=(t == 15),
-            )
-
-        def degree_out(b):
-            lo = (b % 2) * 64
+        def degree_burst(rd):
+            c0, c1 = ROUNDS[rd]
+            bank = psum.tile([P, 512], F32, tag=next_o_tag(), name="deg_%d" % rd)
+            for b in range(c0, c1):
+                for jj in range(2):
+                    lo = ((b - c0) * 2 + jj) * 32
+                    for t in range(16):
+                        tile_, tloc, off = h_at(b, t)
+                        nc.tensor.matmul(
+                            out=bank[:, lo : lo + 32],
+                            lhsT=tile_[:, tloc, off + jj * P : off + (jj + 1) * P],
+                            rhs=ones[:],
+                            start=(t == 0),
+                            stop=(t == 15),
+                        )
             nc.scalar.copy(
-                out=deg_sb[:, b, :], in_=dbank[:, lo : lo + 64].rearrange("p (j n) -> p j n", n=32)[:, :, 0]
+                out=deg_sb[:, c0:c1, :],
+                in_=bank[:, 0 : (c1 - c0) * 64].rearrange("p (c j n) -> p c j n", j=2, n=32)[:, :, :, 0],
             )
 
-        def degree_slot(s, which):
-            finished = []
-            count = DEG_QUOTA.get((s, which), 4 if (s, which) >= DEG_FROM else 0)
-            for n in range(count):
-                if deg_queue:
-                    b, jj, t = deg_queue.pop(0)
-                    degree_matmul(b, jj, t)
-                    if jj == 1 and t == 15:
-                        finished.append(b)
-                else:
-                    tile_, tloc, off = h_at(7, 0)
-                    nc.tensor.matmul(
-                        out=dbank[:, 128:160], lhsT=tile_[:, tloc, off : off + P], rhs=ones[:], start=True, stop=True
-                    )
-            return finished
-
-        def chain(b):
+        def chain(rd):
+            c0, c1 = ROUNDS[rd]
             nc.vector.scalar_tensor_tensor(
-                out=safe_deg[:, b, :], in0=deg_sb[:, b, :], scalar=0.0, in1=deg_sb[:, b, :],
+                out=safe_deg[:, c0:c1, :], in0=deg_sb[:, c0:c1, :], scalar=0.0, in1=deg_sb[:, c0:c1, :],
                 op0=ALU.is_equal, op1=ALU.add,
             )
-            nc.vector.reciprocal(out=recip[:, b, :], in_=safe_deg[:, b, :])
+            nc.vector.reciprocal(out=recip[:, c0:c1, :], in_=safe_deg[:, c0:c1, :])
             nc.vector.scalar_tensor_tensor(
-                out=rhs_sb[:, b, 0, :], in0=deg_sb[:, b, :], scalar=0.0, in1=recip[:, b, :],
+                out=a_pad[:, c0:c1, :], in0=deg_sb[:, c0:c1, :], scalar=0.0, in1=recip[:, c0:c1, :],
                 op0=ALU.is_equal, op1=ALU.subtract,
             )
             nc.vector.tensor_tensor(
-                out=rhs_sb[:, b, 1, :], in0=rhs_sb[:, b, 0, :], in1=rhs_sb[:, b, 0, :], op=ALU.mult
+                out=a_pad[:, 8 + c0 : 8 + c1, :], in0=a_pad[:, c0:c1, :], in1=a_pad[:, c0:c1, :], op=ALU.mult
             )
 
-        def select(b):
-            bank = psum.tile([P, 512], F32, tag=next_o_tag(), name="sel_%d" % b)
-            for par in range(2):
-                nc.tensor.matmul(
-                    out=bank[:, par * 4 : (par + 1) * 4],
-                    lhsT=nsel[par][:],
-                    rhs=rhs_sb[:, b, :, :].rearrange("p k j -> p (k j)"),
-                    start=True,
-                    stop=True,
-                )
-            selbank[b] = bank
+        def to_rows(rd):
+            bank = psum.tile([P, 512], F32, tag=next_o_tag(), name="rows_%d" % rd)
+            for jj in range(2):
+                nc.tensor.transpose(bank[:, jj * P : (jj + 1) * P], a_pad[:, :, jj], ident[:])
+            selbank[("r", rd)] = bank
 
-        def half_copies(b):
-            for hf in range(2):
-                rows = slice(hf * 64, (hf + 1) * 64)
-                src = selbank[b][rows, 0:8].rearrange("q (r k j) -> q r k j", r=2, k=2, j=2)
-                nc.scalar.copy(out=scal[rows, b, :, :], in_=src[:, :, :, hf])
+        def rows_copy(rd):
+            nc.scalar.copy(out=r_sb[:], in_=selbank[("r", rd)][:, 0:256])
+
+        def to_parity(rd):
+            bank = psum.tile([P, 2, P], F32, tag=next_o_tag(), name="par_%d" % rd)
+            rview = r_sb[:].rearrange("c (q r) -> c q r", r=2)
+            for par in range(2):
+                nc.tensor.transpose(bank[:, par, :], rview[:, :, par], ident[:])
+            selbank[("p", rd)] = bank
+
+        def scal_copy(rd):
+            c0, c1 = ROUNDS[rd]
+            src = selbank[("p", rd)][:, :, 0:16].rearrange("q r (k c) -> q r k c", k=2)
+            nc.scalar.mul(
+                out=scal[:, c0:c1, :, :].rearrange("q c r k -> q r k c"), in_=src[:, :, :, c0:c1], mul=-1.0
+            )
 
         def make_bias(b):
             nc.vector.tensor_reduce(out=csum[:, b, :], in_=c4[:, b, :, :], axis=AX.X, op=ALU.add)
@@ -396,17 +375,16 @@ def tile_v2emsgpass_kernel(tc, X, H, grad_out, out):
         ptcopy(2)
         h_transposes(2)
         weighted_sums(2)
-        for jj in range(2):
-            for t in range(16):
-                degree_matmul(0, jj, t)
-        degree_out(0)
+        degree_burst(0)
         chain(0)
         mx(3)
         ptcopy(3)
         h_transposes(3)
         h_transposes(4)
-        select(0)
-        half_copies(0)
+        to_rows(0)
+        rows_copy(0)
+        to_parity(0)
+        scal_copy(0)
         weighted_sums(3)
         make_bias(0)
         affine(0)
@@ -414,15 +392,13 @@ def tile_v2emsgpass_kernel(tc, X, H, grad_out, out):
         for s in range(4, 32 + OT_LAG):
             if s < 32:
                 mx(s)
-                finished = degree_slot(s, "A")
                 ptcopy(s)
-                for b in finished:
-                    degree_out(b)
-                    chain_at[s] = b
-                    select_at[s + 1] = b
-                    half_at[s + 2] = b
-            if s in half_at:
-                half_copies(half_at[s])
+            if s - 2 in BURST_AT:
+                rows_copy(BURST_AT[s - 2])
+            if s - 3 in BURST_AT:
+                scal_copy(BURST_AT[s - 3])
+            if s in BURST_AT:
+                degree_burst(BURST_AT[s])
             todo = [idx for idx in ((s - OT_LAG) * 2, (s - OT_LAG) * 2 + 1) if 0 <= idx < 64]
             for idx in todo:
                 back_transposes(idx)
@@ -432,10 +408,12 @@ def tile_v2emsgpass_kernel(tc, X, H, grad_out, out):
                 weighted_sums(s)
             for idx in todo:
                 out_copy(idx)
-            if s in chain_at:
-                chain(chain_at[s])
-            if s in select_at:
-                select(select_at[s])
+            if s in BURST_AT:
+                chain(BURST_AT[s])
+            if s - 1 in BURST_AT:
+                to_rows(BURST_AT[s - 1])
+            if s - 2 in BURST_AT:
+                to_parity(BURST_AT[s - 2])
             if s < 32 and s % 4 == 3:
                 make_bias(s // 4)
                 affine(s // 4)
@@ -446,6 +424,3 @@ def tile_v2emsgpass_kernel(tc, X, H, grad_out, out):
                 prep_copy("g", i, 1, "V")
             if s - 1 in GPREP_AT:
                 quantise("g", GPREP_AT[s - 1])
-            if s < 32:
-                late = degree_slot(s, "B")
-                assert not late

@@ -60,7 +60,7 @@ def tile_v2emsgpass_kernel(tc, X, H, grad_out, out):
         nc.vector.memset(a_pad[:], 0.0)
         r_sb = const.tile([P, 256], F32, name="r_sb")
 
-        junk = const.tile([P, 512], F32, name="junk")
+        junk = [const.tile([P, 512], F32, name="junk%d" % i) for i in range(3)]
         deg_sb = const.tile([P, 8, 2], F32, name="deg_sb")
         safe_deg = const.tile([P, 8, 2], F32, name="safe_deg")
         recip = const.tile([P, 8, 2], F32, name="recip")
@@ -191,7 +191,7 @@ def tile_v2emsgpass_kernel(tc, X, H, grad_out, out):
             hview = ht[s][:].bitcast(BF16).rearrange("q (n r) -> q n r", r=2)
             for par in range(2):
                 nc.vector.scalar_tensor_tensor(
-                    out=junk[:],
+                    out=junk[(2 * s + par) % 3][:],
                     in0=hview[:, :, par],
                     scalar=1.0,
                     in1=ptsb[b][:, par, nb * 512 : (nb + 1) * 512],

@@ -29,7 +29,7 @@ ROUNDS = ((0, 1), (1, 2), (2, 4), (4, 8))
 BURST_AT = {4: 1, 7: 2, 14: 3}
 GPREP_AT = {4: 1, 9: 2, 11: 3}
 OT_LAG = 6
-V_COPIES = (1, 5)
+V_COPIES = (1, 3, 5, 7)
 TAIL_IDX = 52
 TAIL_TAGS = ("o0", "o1", "o2", "pt0", "pt1")
 SPLIT_PAIRS = (2, 3)

@@ -26,12 +26,11 @@ H_CHUNKS = (
     (0, 16, 1024, 2048),
 )
 ROUNDS = ((0, 1), (1, 2), (2, 4), (4, 8))
-BURST_AT = {4: 1, 7: 2, 14: 3}
-GPREP_AT = {4: 1, 9: 2, 11: 3}
-OT_LAG = 6
-V_COPIES = (1, 3, 5, 7)
+BURST_AT = {2: 1, 4: 2, 7: 3}
+GPREP_AT = {2: 1, 5: 2, 6: 3}
+OT_LAG = 3
 TAIL_IDX = 52
-TAIL_TAGS = ("o0", "o1", "o2", "pt0", "pt1")
+TAIL_TAGS = ("w0", "w1", "w2", "w3", "ht0", "ht1", "ht2", "ht3")
 SPLIT_PAIRS = (2, 3)
 
 
@@ -91,7 +90,7 @@ def tile_v2emsgpass_kernel(tc, X, H, grad_out, out):
         uses = [0]
 
         def next_o_tag():
-            tag = "o%d" % (uses[0] % 3)
+            tag = "w%d" % (uses[0] % 4)
             uses[0] = uses[0] + 1
             return tag
 
@@ -154,7 +153,7 @@ def tile_v2emsgpass_kernel(tc, X, H, grad_out, out):
         def mx(s):
             b, nb = divmod(s, 4)
             for par in range(2):
-                bank = psum.tile([P, 512], F32, tag="pt%d" % par, name="pt_%d_%d" % (s, par))
+                bank = psum.tile([P, 512], F32, tag=next_o_tag(), name="pt_%d_%d" % (s, par))
                 ecols = slice(b * 256 + par * P, b * 256 + (par + 1) * P)
                 ncols = slice(nb * 512, (nb + 1) * 512)
                 nc.tensor.matmul_mx(
@@ -177,7 +176,7 @@ def tile_v2emsgpass_kernel(tc, X, H, grad_out, out):
 
         def h_transposes(u):
             b, nb = divmod(u, 4)
-            bank = psum.tile([P, 512], F32, tag="ht%d" % (u % 3), name="ht_%d" % u)
+            bank = psum.tile([P, 512], F32, tag="ht%d" % (u % 4), name="ht_%d" % u)
             for tl in range(4):
                 tile_, tloc, off = h_at(b, 4 * nb + tl)
                 words = tile_[:].bitcast(F32)
@@ -290,7 +289,7 @@ def tile_v2emsgpass_kernel(tc, X, H, grad_out, out):
 
         def back_transposes(idx):
             b, k = divmod(idx, 8)
-            tag = next_o_tag() if idx < TAIL_IDX else TAIL_TAGS[idx % 5]
+            tag = next_o_tag() if idx < TAIL_IDX else TAIL_TAGS[idx % 8]
             bank = psum.tile([P, 2, 2, P], F32, tag=tag, name="o_%d" % idx)
             for tl in range(2):
                 for par in range(2):
@@ -307,7 +306,7 @@ def tile_v2emsgpass_kernel(tc, X, H, grad_out, out):
             b, k = divmod(idx, 8)
             pair, half = divmod(b, 2)
             if idx < TAIL_IDX:
-                engine = "V" if idx % 8 in V_COPIES else "S"
+                engine = "V" if idx % 4 == 0 else "S"
             elif idx < TAIL_IDX + 6:
                 engine = "S"
             else:
@@ -341,7 +340,7 @@ def tile_v2emsgpass_kernel(tc, X, H, grad_out, out):
         load_h(2)
         prep_copy("x", 0, 0, "S")
         prep_copy("x", 0, 1, "V")
-        prep_transposes("g", 0, ("pt0", "pt1"))
+        prep_transposes("g", 0, None)
         load_rows("g", 1)
         load_h(3)
         prep_copy("g", 0, 0, "S")
@@ -351,76 +350,66 @@ def tile_v2emsgpass_kernel(tc, X, H, grad_out, out):
         load_rows("g", 2)
         quantise("g", 0)
         prep_copy("x", 1, 0, "S")
-        prep_copy("x", 1, 1, "S")
-        quantise("x", 1)
-        mx(0)
-        ptcopy(0)
+        prep_copy("x", 1, 1, "V")
         h_transposes(0)
         h_transposes(1)
-        weighted_sums(0)
+        quantise("x", 1)
         prep_transposes("x", 2, None)
         load_rows("g", 3)
         load_h(4)
         prep_copy("x", 2, 0, "S")
         prep_copy("x", 2, 1, "S")
         quantise("x", 2)
-        mx(1)
-        ptcopy(1)
-        weighted_sums(1)
-        prep_transposes("x", 3, None)
-        prep_copy("x", 3, 0, "S")
-        prep_copy("x", 3, 1, "S")
-        quantise("x", 3)
-        mx(2)
-        ptcopy(2)
-        h_transposes(2)
-        weighted_sums(2)
-        degree_burst(0)
-        chain(0)
-        mx(3)
-        ptcopy(3)
-        h_transposes(3)
-        h_transposes(4)
-        to_rows(0)
-        rows_copy(0)
-        to_parity(0)
-        scal_copy(0)
-        weighted_sums(3)
-        make_bias(0)
-        affine(0)
 
-        for s in range(4, 32 + OT_LAG):
-            if s < 32:
-                mx(s)
-                ptcopy(s)
-            if s - 2 in BURST_AT:
-                rows_copy(BURST_AT[s - 2])
-            if s - 3 in BURST_AT:
-                scal_copy(BURST_AT[s - 3])
-            if s in BURST_AT:
-                degree_burst(BURST_AT[s])
-            todo = [idx for idx in ((s - OT_LAG) * 2, (s - OT_LAG) * 2 + 1) if 0 <= idx < 64]
-            for idx in todo:
+        started = {0: 0, 2: 1, 4: 2, 7: 3}
+        for g in range(16 + OT_LAG):
+            if g < 16:
+                mx(2 * g)
+                mx(2 * g + 1)
+                ptcopy(2 * g)
+                ptcopy(2 * g + 1)
+            if g - 1 in started:
+                to_rows(started[g - 1])
+                rows_copy(started[g - 1])
+            if g == 0:
+                prep_transposes("x", 3, None)
+                prep_copy("x", 3, 0, "S")
+                prep_copy("x", 3, 1, "S")
+            if g in BURST_AT:
+                degree_burst(BURST_AT[g])
+            todo = [idx for idx in range(4 * (g - OT_LAG), 4 * (g - OT_LAG) + 4) if 0 <= idx < 64]
+            for idx in todo[:2]:
                 back_transposes(idx)
-            if s + 1 < 32:
-                h_transposes(s + 1)
-            if s < 32:
-                weighted_sums(s)
-            for idx in todo:
+            if 2 * g + 2 < 32:
+                h_transposes(2 * g + 2)
+            if g < 16:
+                weighted_sums(2 * g)
+            if g == 0:
+                quantise("x", 3)
+            for idx in todo[:2]:
                 out_copy(idx)
-            if s in BURST_AT:
-                chain(BURST_AT[s])
-            if s - 1 in BURST_AT:
-                to_rows(BURST_AT[s - 1])
-            if s - 2 in BURST_AT:
-                to_parity(BURST_AT[s - 2])
-            if s < 32 and s % 4 == 3:
-                make_bias(s // 4)
-                affine(s // 4)
-            if s in GPREP_AT:
-                i = GPREP_AT[s]
+            for idx in todo[2:]:
+                back_transposes(idx)
+            if 2 * g + 3 < 32:
+                h_transposes(2 * g + 3)
+            if g == 0:
+                degree_burst(0)
+            if g < 16:
+                weighted_sums(2 * g + 1)
+            for idx in todo[2:]:
+                out_copy(idx)
+            if g in started:
+                chain(started[g])
+            if g - 1 in started:
+                to_parity(started[g - 1])
+                scal_copy(started[g - 1])
+            if g < 16 and g % 2 == 1:
+                make_bias(g // 2)
+                affine(g // 2)
+            if g in GPREP_AT:
+                i = GPREP_AT[g]
                 prep_transposes("g", i, None)
                 prep_copy("g", i, 0, "S")
                 prep_copy("g", i, 1, "V")
-            if s - 1 in GPREP_AT:
-                quantise("g", GPREP_AT[s - 1])
+            if g - 1 in GPREP_AT:
+                quantise("g", GPREP_AT[g - 1])

@@ -306,7 +306,7 @@ def tile_v2emsgpass_kernel(tc, X, H, grad_out, out):
             b, k = divmod(idx, 8)
             pair, half = divmod(b, 2)
             if idx < TAIL_IDX:
-                engine = "V" if idx % 4 == 0 else "S"
+                engine = "V" if idx % 8 in (0, 1, 4) else "S"
             elif idx < TAIL_IDX + 6:
                 engine = "S"
             else:

from contextlib import ExitStack

import concourse.mybir as mybir
from concourse.masks import make_identity

F32 = mybir.dt.float32
BF16 = mybir.dt.bfloat16
U32 = mybir.dt.uint32
U8 = mybir.dt.uint8
E4M3X4 = mybir.dt.float8_e4m3fn_x4
E5M2X4 = mybir.dt.float8_e5m2_x4
ALU = mybir.AluOpType
AX = mybir.AxisListType

P = 128
NV = 2048
NE = 2048
D = 512
FLOPS = 2 * NV * NE * D

H_CHUNKS = (
    (0, 8, 0, 256),
    (8, 16, 0, 256),
    (0, 16, 256, 512),
    (0, 16, 512, 1024),
    (0, 16, 1024, 2048),
)
ROUNDS = ((0, 1), (1, 2), (2, 4), (4, 8))
BURST_AT = {2: 1, 4: 2, 7: 3}
GPREP_AT = {2: 1, 5: 2, 6: 3}
OT_LAG = 3
TAIL_IDX = 52
TAIL_TAGS = ("w0", "w1", "w2", "w3", "ht0", "ht1", "ht2", "ht3")
SPLIT_PAIRS = (2, 3)


def tile_v2emsgpass_kernel(tc, X, H, grad_out, out):
    nc = tc.nc
    with ExitStack() as ctx:
        const = ctx.enter_context(tc.tile_pool(name="const", bufs=1))
        hpool = ctx.enter_context(tc.tile_pool(name="hpool", bufs=1))
        rawp = ctx.enter_context(tc.tile_pool(name="rawp", bufs=4))
        grpp = ctx.enter_context(tc.tile_pool(name="grpp", bufs=3))
        ptp = ctx.enter_context(tc.tile_pool(name="ptp", bufs=3))
        outp = ctx.enter_context(tc.tile_pool(name="outp", bufs=2))
        psum = ctx.enter_context(tc.psum_pool(name="psum", bufs=1))
        ctx.enter_context(tc.manual_schedule())

        xv = X.rearrange("(p t) d -> p t d", t=16)
        gv = grad_out.rearrange("(b q r) d -> q b r d", q=P, r=2)
        hv = H.rearrange("(p t) e -> p t e", t=16)
        ov = out.rearrange("(p t) e -> p t e", t=16)

        ident = const.tile([P, P], F32, name="ident")
        make_identity(nc, ident[:])
        ones = const.tile([P, 32], BF16, name="ones")
        nc.vector.memset(ones[:], 1.0)
        a_pad = const.tile([P, P, 2], F32, name="a_pad")
        nc.vector.memset(a_pad[:], 0.0)
        r_sb = const.tile([P, 256], F32, name="r_sb")

        junk = [const.tile([P, 512], F32, name="junk%d" % i) for i in range(3)]
        deg_sb = const.tile([P, 8, 2], F32, name="deg_sb")
        safe_deg = const.tile([P, 8, 2], F32, name="safe_deg")
        recip = const.tile([P, 8, 2], F32, name="recip")
        scal = const.tile([P, 8, 2, 2], F32, name="scal")
        c4 = const.tile([P, 8, 2, 4], F32, name="c4")
        csum = const.tile([P, 8, 2], F32, name="csum")
        bias = const.tile([P, 8, 2], F32, name="bias")
        codes = {
            "x": const.tile([P, NV], U32, name="x_codes", align_bytes=64),
            "g": const.tile([P, NE], U32, name="g_codes", align_bytes=64),
        }
        scales = {
            "x": const.tile([P, NV], U8, name="x_scales", align_bytes=64),
            "g": const.tile([P, NE], U8, name="g_scales", align_bytes=64),
        }
        fmt = {"x": E4M3X4, "g": E5M2X4}

        raw = {}
        grouped = {}
        prep_bank = {}
        h_tiles = {}
        pt = {}
        ht = {}
        ptsb = {}
        obank = {}
        osb = {}
        selbank = {}
        uses = [0]

        def next_o_tag():
            tag = "w%d" % (uses[0] % 4)
            uses[0] = uses[0] + 1
            return tag

        def evac(engine, dst, src):
            if engine == "S":
                nc.scalar.copy(out=dst, in_=src)
            else:
                nc.vector.tensor_copy(out=dst, in_=src)

        def load_rows(kind, i):
            t = rawp.tile([P, 4, D], BF16, name="raw_%s%d" % (kind, i), tag="raw")
            if kind == "x":
                nc.sync.dma_start(out=t[:], in_=xv[:, 4 * i : 4 * i + 4, :])
            else:
                nc.sync.dma_start(
                    out=t[:].rearrange("q (b r) d -> q b r d", b=2),
                    in_=gv[:, 2 * i : 2 * i + 2, :, :],
                )
            raw[(kind, i)] = t

        def load_h(i):
            t0, t1, e0, e1 = H_CHUNKS[i]
            t = hpool.tile([P, t1 - t0, e1 - e0], BF16, name="h%d" % i)
            nc.sync.dma_start(out=t[:], in_=hv[:, t0:t1, e0:e1])
            h_tiles[i] = t

        def h_at(b, t):
            found = None
            for i, (t0, t1, e0, e1) in enumerate(H_CHUNKS):
                if t0 <= t < t1 and e0 <= 256 * b < e1:
                    found = (h_tiles[i], t - t0, 256 * b - e0)
            return found

        def prep_transposes(kind, i, tags):
            words = raw[(kind, i)][:].bitcast(F32)
            for h in range(2):
                tag = tags[h] if tags else next_o_tag()
                bank = psum.tile([P, 2, 2, P], F32, tag=tag, name="prep_%s%d_%d" % (kind, i, h))
                for r in range(2):
                    for u in range(2):
                        nc.tensor.transpose(bank[:, r, u, :], words[:, 2 * h + r, u * P : (u + 1) * P], ident[:])
                prep_bank[(kind, i, h)] = bank

        def prep_copy(kind, i, h, engine):
            if h == 0:
                grouped[(kind, i)] = grpp.tile(
                    [P, 2048], BF16, name="grp_%s%d" % (kind, i), tag="grp", align_bytes=64
                )
            dst = grouped[(kind, i)][:].bitcast(F32).rearrange("w (r c u) -> w r c u", r=4, u=2)
            evac(engine, dst[:, 2 * h : 2 * h + 2], prep_bank[(kind, i, h)][:].rearrange("w r u c -> w r c u"))

        def quantise(kind, i):
            cols = slice(i * 512, (i + 1) * 512)
            nc.vector.quantize_mx(
                out=codes[kind][:, cols].bitcast(fmt[kind]),
                scales=scales[kind][:, cols],
                in_=grouped[(kind, i)][:],
            )

        def mx(s):
            b, nb = divmod(s, 4)
            for par in range(2):
                bank = psum.tile([P, 512], F32, tag=next_o_tag(), name="pt_%d_%d" % (s, par))
                ecols = slice(b * 256 + par * P, b * 256 + (par + 1) * P)
                ncols = slice(nb * 512, (nb + 1) * 512)
                nc.tensor.matmul_mx(
                    out=bank[:],
                    lhsT=codes["g"][:, ecols].bitcast(E5M2X4),
                    lhsT_scale=scales["g"][:, ecols],
                    rhs=codes["x"][:, ncols].bitcast(E4M3X4),
                    rhs_scale=scales["x"][:, ncols],
                    start=True,
                    stop=True,
                )
                pt[(s, par)] = bank

        def ptcopy(s):
            b, nb = divmod(s, 4)
            if nb == 0:
                ptsb[b] = ptp.tile([P, 2, NV], F32, name="ptsb%d" % b, tag="ptsb")
            for par in range(2):
                nc.scalar.copy(out=ptsb[b][:, par, nb * 512 : (nb + 1) * 512], in_=pt[(s, par)][:])

        def h_transposes(u):
            b, nb = divmod(u, 4)
            bank = psum.tile([P, 512], F32, tag="ht%d" % (u % 4), name="ht_%d" % u)
            for tl in range(4):
                tile_, tloc, off = h_at(b, 4 * nb + tl)
                words = tile_[:].bitcast(F32)
                nc.tensor.transpose(
                    bank[:, tl * P : (tl + 1) * P], words[:, tloc, off // 2 : off // 2 + P], ident[:]
                )
            ht[u] = bank

        def weighted_sums(s):
            b, nb = divmod(s, 4)
            hview = ht[s][:].bitcast(BF16).rearrange("q (n r) -> q n r", r=2)
            for par in range(2):
                nc.vector.scalar_tensor_tensor(
                    out=junk[(2 * s + par) % 3][:],
                    in0=hview[:, :, par],
                    scalar=1.0,
                    in1=ptsb[b][:, par, nb * 512 : (nb + 1) * 512],
                    op0=ALU.mult,
                    op1=ALU.mult,
                    accum_out=c4[:, b, par, nb : nb + 1],
                )

        def degree_burst(rd):
            c0, c1 = ROUNDS[rd]
            bank = psum.tile([P, 512], F32, tag=next_o_tag(), name="deg_%d" % rd)
            for b in range(c0, c1):
                for jj in range(2):
                    lo = ((b - c0) * 2 + jj) * 32
                    for t in range(16):
                        tile_, tloc, off = h_at(b, t)
                        nc.tensor.matmul(
                            out=bank[:, lo : lo + 32],
                            lhsT=tile_[:, tloc, off + jj * P : off + (jj + 1) * P],
                            rhs=ones[:],
                            start=(t == 0),
                            stop=(t == 15),
                        )
            nc.scalar.copy(
                out=deg_sb[:, c0:c1, :],
                in_=bank[:, 0 : (c1 - c0) * 64].rearrange("p (c j n) -> p c j n", j=2, n=32)[:, :, :, 0],
            )

        def chain(rd):
            c0, c1 = ROUNDS[rd]
            nc.vector.scalar_tensor_tensor(
                out=safe_deg[:, c0:c1, :], in0=deg_sb[:, c0:c1, :], scalar=0.0, in1=deg_sb[:, c0:c1, :],
                op0=ALU.is_equal, op1=ALU.add,
            )
            nc.vector.reciprocal(out=recip[:, c0:c1, :], in_=safe_deg[:, c0:c1, :])
            nc.vector.scalar_tensor_tensor(
                out=a_pad[:, c0:c1, :], in0=deg_sb[:, c0:c1, :], scalar=0.0, in1=recip[:, c0:c1, :],
                op0=ALU.is_equal, op1=ALU.subtract,
            )
            nc.vector.tensor_tensor(
                out=a_pad[:, 8 + c0 : 8 + c1, :], in0=a_pad[:, c0:c1, :], in1=a_pad[:, c0:c1, :], op=ALU.mult
            )

        def to_rows(rd):
            bank = psum.tile([P, 512], F32, tag=next_o_tag(), name="rows_%d" % rd)
            for jj in range(2):
                nc.tensor.transpose(bank[:, jj * P : (jj + 1) * P], a_pad[:, :, jj], ident[:])
            selbank[("r", rd)] = bank

        def rows_copy(rd):
            nc.scalar.copy(out=r_sb[:], in_=selbank[("r", rd)][:, 0:256])

        def to_parity(rd):
            bank = psum.tile([P, 2, P], F32, tag=next_o_tag(), name="par_%d" % rd)
            rview = r_sb[:].rearrange("c (q r) -> c q r", r=2)
            for par in range(2):
                nc.tensor.transpose(bank[:, par, :], rview[:, :, par], ident[:])
            selbank[("p", rd)] = bank

        def scal_copy(rd):
            c0, c1 = ROUNDS[rd]
            src = selbank[("p", rd)][:, :, 0:16].rearrange("q r (k c) -> q r k c", k=2)
            nc.scalar.mul(
                out=scal[:, c0:c1, :, :].rearrange("q c r k -> q r k c"), in_=src[:, :, :, c0:c1], mul=-1.0
            )

        def make_bias(b):
            nc.vector.tensor_reduce(out=csum[:, b, :], in_=c4[:, b, :, :], axis=AX.X, op=ALU.add)
            nc.vector.tensor_tensor(out=bias[:, b, :], in0=csum[:, b, :], in1=scal[:, b, :, 1], op=ALU.mult)

        def affine(b):
            if b < 7:
                for h in range(2):
                    for par in range(2):
                        seg = ptsb[b][:, par, h * 1024 : (h + 1) * 1024]
                        nc.gpsimd.tensor_scalar(
                            out=seg,
                            in0=seg,
                            scalar1=scal[:, b, par, 0:1],
                            scalar2=bias[:, b, par : par + 1],
                            op0=ALU.mult,
                            op1=ALU.add,
                        )
            else:
                for h in range(4):
                    for par in range(2):
                        seg = ptsb[b][:, par, h * 512 : (h + 1) * 512]
                        nc.vector.tensor_scalar(
                            out=seg,
                            in0=seg,
                            scalar1=scal[:, b, par, 0:1],
                            scalar2=bias[:, b, par : par + 1],
                            op0=ALU.mult,
                            op1=ALU.add,
                        )

        def back_transposes(idx):
            b, k = divmod(idx, 8)
            tag = next_o_tag() if idx < TAIL_IDX else TAIL_TAGS[idx % 8]
            bank = psum.tile([P, 2, 2, P], F32, tag=tag, name="o_%d" % idx)
            for tl in range(2):
                for par in range(2):
                    t = 2 * k + tl
                    nc.tensor.transpose(bank[:, tl, par, :], ptsb[b][:, par, t * P : (t + 1) * P], ident[:])
            obank[idx] = bank

        def store(pair, t0, t1, c0, c1):
            nc.sync.dma_start(
                out=ov[:, t0:t1, pair * 512 + c0 : pair * 512 + c1], in_=osb[pair][:, t0:t1, c0:c1]
            )

        def out_copy(idx):
            b, k = divmod(idx, 8)
            pair, half = divmod(b, 2)
            if idx < TAIL_IDX:
                engine = "V" if idx % 8 in (0, 1, 4) else "S"
            elif idx < TAIL_IDX + 6:
                engine = "S"
            else:
                engine = "V" if idx % 2 == 0 else "S"
            if half == 0 and k == 0:
                osb[pair] = outp.tile([P, 16, 512], F32, name="osb%d" % pair, tag="osb")
            dst = osb[pair][:, 2 * k : 2 * k + 2, half * 256 : (half + 1) * 256]
            evac(engine, dst.rearrange("p t (q r) -> p t q r", r=2), obank[idx][:].rearrange("p t r q -> p t q r"))
            c0 = half * 256
            if pair in SPLIT_PAIRS:
                if b < 7:
                    if k in (3, 7):
                        store(pair, 2 * k - 6, 2 * k + 2, c0, c0 + 256)
                else:
                    if k in (1, 3, 5):
                        store(pair, 2 * k - 2, 2 * k + 2, c0, c0 + 256)
                    if k in (6, 7):
                        store(pair, 2 * k, 2 * k + 2, c0, c0 + 256)
            elif half == 1:
                if k in (3, 7):
                    store(pair, 2 * k - 6, 2 * k + 2, 0, 512)

        load_rows("x", 0)
        load_rows("g", 0)
        load_rows("x", 1)
        load_h(0)
        load_rows("x", 2)
        prep_transposes("x", 0, None)
        load_rows("x", 3)
        load_h(1)
        load_h(2)
        prep_copy("x", 0, 0, "S")
        prep_copy("x", 0, 1, "V")
        prep_transposes("g", 0, None)
        load_rows("g", 1)
        load_h(3)
        prep_copy("g", 0, 0, "S")
        prep_copy("g", 0, 1, "V")
        quantise("x", 0)
        prep_transposes("x", 1, None)
        load_rows("g", 2)
        quantise("g", 0)
        prep_copy("x", 1, 0, "S")
        prep_copy("x", 1, 1, "V")
        h_transposes(0)
        h_transposes(1)
        quantise("x", 1)
        prep_transposes("x", 2, None)
        load_rows("g", 3)
        load_h(4)
        prep_copy("x", 2, 0, "S")
        prep_copy("x", 2, 1, "S")
        quantise("x", 2)

        started = {0: 0, 2: 1, 4: 2, 7: 3}
        for g in range(16 + OT_LAG):
            if g < 16:
                mx(2 * g)
                mx(2 * g + 1)
                ptcopy(2 * g)
                ptcopy(2 * g + 1)
            if g - 1 in started:
                to_rows(started[g - 1])
                rows_copy(started[g - 1])
            if g == 0:
                prep_transposes("x", 3, None)
                prep_copy("x", 3, 0, "S")
                prep_copy("x", 3, 1, "S")
            if g in BURST_AT:
                degree_burst(BURST_AT[g])
            todo = [idx for idx in range(4 * (g - OT_LAG), 4 * (g - OT_LAG) + 4) if 0 <= idx < 64]
            for idx in todo[:2]:
                back_transposes(idx)
            if 2 * g + 2 < 32:
                h_transposes(2 * g + 2)
            if g < 16:
                weighted_sums(2 * g)
            if g == 0:
                quantise("x", 3)
            for idx in todo[:2]:
                out_copy(idx)
            for idx in todo[2:]:
                back_transposes(idx)
            if 2 * g + 3 < 32:
                h_transposes(2 * g + 3)
            if g == 0:
                degree_burst(0)
            if g < 16:
                weighted_sums(2 * g + 1)
            for idx in todo[2:]:
                out_copy(idx)
            if g in started:
                chain(started[g])
            if g - 1 in started:
                to_parity(started[g - 1])
                scal_copy(started[g - 1])
            if g < 16 and g % 2 == 1:
                make_bias(g // 2)
                affine(g // 2)
            if g in GPREP_AT:
                i = GPREP_AT[g]
                prep_transposes("g", i, None)
                prep_copy("g", i, 0, "S")
                prep_copy("g", i, 1, "V")
            if g - 1 in GPREP_AT:
                quantise("g", GPREP_AT[g - 1])
